import numpy as np
import ml_dtypes


def mxq(x, axis, fmt="e4m3"):
    dtype, down = {"e4m3": (ml_dtypes.float8_e4m3fn, 7), "e5m2": (ml_dtypes.float8_e5m2, 14)}[fmt]
    v = np.moveaxis(np.asarray(x, np.float32).astype(ml_dtypes.bfloat16).astype(np.float64), axis, -1)
    blocks = v.reshape(v.shape[:-1] + (-1, 32))
    amax = np.abs(blocks).max(-1, keepdims=True)
    byte = np.maximum(np.where(amax > 0, np.frexp(amax)[1] - 1 + 127, 0) - down, 1)
    scale = np.exp2(byte - 127.0)
    codes = (blocks / scale).astype(np.float32).astype(dtype).astype(np.float64)
    return np.moveaxis((codes * scale).reshape(v.shape), -1, axis)


WIDE = False


def mx_kscale(k):
    if not WIDE:
        return np.ones(k)
    levels = np.array([10, -10, 5, -5, 0])
    a = np.random.permutation(np.resize(levels, k // 512 * 4)).reshape(k // 512, 4)
    idx = np.arange(k)
    return np.exp2(a[idx // 512, idx % 128 // 32])


BF16 = ml_dtypes.bfloat16


def bf(x):
    return np.asarray(x, np.float32).astype(BF16)


def f64(x):
    return np.asarray(x).astype(np.float64)


B, C, H, W, RQ, RV = 1, 2048, 64, 32, 8, 2
DQ, DV = C // RQ, C // RV
N = H * W


def maxpool2(x):
    b, c, h, w = x.shape
    return x.reshape(b, c, h // 2, 2, w // 2, 2).max(axis=(3, 5))


def setup_inputs():
    s = mx_kscale(C)
    return {"imgs": bf(np.random.standard_normal((B, C, H, W)) * s[None, :, None, None]),
            "w_kv": bf(np.random.standard_normal((DQ + DV, C)) * 0.5 / np.sqrt(C) / s[None, :])}


def reference(imgs, w_kv):
    x = f64(imgs).reshape(B, C, N)
    kv = (mxq(f64(w_kv), 1, "e4m3") @ mxq(x, 1, "e4m3")).reshape(B, DQ + DV, H, W)
    return maxpool2(kv[:, :DQ]), maxpool2(kv[:, DQ:])

@@ -1,0 +1,145 @@
+from contextlib import ExitStack
+
+import concourse.mybir as mybir
+from concourse.masks import make_identity
+
+F32 = mybir.dt.float32
+BF16 = mybir.dt.bfloat16
+U32 = mybir.dt.uint32
+U8 = mybir.dt.uint8
+FP8X4 = mybir.dt.float8_e4m3fn_x4
+
+P = 128
+C_IN = 2048
+N_PIX = 2048
+O_ALL = 1280
+O_KEYS = 256
+PASSES = 4
+CHUNK = 512
+CHUNKS = 4
+M_TILES = 10
+FIRST_ROUND = 8
+V_COLS = (320, 256, 64, 0)
+
+FLOPS = 2 * O_ALL * C_IN * N_PIX
+
+
+def tile_selfattentionconv2d_pa_kernel(tc, imgs, w_kv, out_0, out_1):
+    nc = tc.nc
+    x_view = imgs.rearrange("b c h w -> (b c) (h w)").rearrange(
+        "(g u q e) n -> g u q e n", g=PASSES, u=2, q=P, e=2
+    )
+    keys_out = out_0.rearrange("b o i j -> (b o) (i j)")
+    vals_out = out_1.rearrange("b o i j -> (b o) (i j)")
+
+    with ExitStack() as ctx:
+        const = ctx.enter_context(tc.tile_pool(name="const", bufs=1))
+        raw = ctx.enter_context(tc.tile_pool(name="raw", bufs=1))
+        keep = ctx.enter_context(tc.tile_pool(name="keep", bufs=1))
+        stage_w = ctx.enter_context(tc.tile_pool(name="stage_w", bufs=3))
+        stage_x = ctx.enter_context(tc.tile_pool(name="stage_x", bufs=4))
+        psum = ctx.enter_context(tc.psum_pool(name="psum", bufs=8))
+
+        ident = const.tile([P, P], F32, name="ident")
+        make_identity(nc, ident[:])
+
+        w_raw = []
+        for m in range(M_TILES):
+            t = raw.tile([P, C_IN], BF16, name="w_raw%d" % m)
+            nc.sync.dma_start(out=t[:], in_=w_kv[m * P : (m + 1) * P, :])
+            w_raw.append(t)
+        x_raw = {}
+        for c in range(CHUNKS):
+            for g in range(PASSES):
+                t = raw.tile([P, 4, CHUNK], BF16, name="x_raw%d_%d" % (c, g))
+                for u in range(2):
+                    nc.sync.dma_start(
+                        out=t[:, 2 * u : 2 * u + 2, :],
+                        in_=x_view[g, u, :, :, c * CHUNK : (c + 1) * CHUNK],
+                    )
+                x_raw[(c, g)] = t
+
+        w_codes = []
+        w_scales = []
+        for m in range(M_TILES):
+            words = w_raw[m][:].bitcast(F32)
+            wg = stage_w.tile([P, C_IN], BF16, name="wg", tag="wg", align_bytes=64)
+            wg_words = wg[:].bitcast(F32).rearrange("p (g o u) -> p g o u", g=PASSES, o=P, u=2)
+            for h in range(2):
+                bank = psum.tile([P, 512], F32, name="tp", tag="bank")
+                for j in range(4):
+                    col = (4 * h + j) * P
+                    nc.tensor.transpose(bank[:, j * P : (j + 1) * P], words[:, col : col + P], ident[:])
+                nc.scalar.copy(
+                    out=wg_words[:, 2 * h : 2 * h + 2, :, :],
+                    in_=bank[:].rearrange("p (g u o) -> p g o u", g=2, u=2, o=P),
+                )
+            wc = keep.tile([P, PASSES * P], U32, name="wc%d" % m, align_bytes=64)
+            ws = keep.tile([P, PASSES * P], U8, name="ws%d" % m, align_bytes=64)
+            nc.vector.quantize_mx(out=wc[:].bitcast(FP8X4), scales=ws[:], in_=wg[:])
+            w_codes.append(wc)
+            w_scales.append(ws)
+
+        x_codes = {}
+        x_scales = {}
+        for c in range(CHUNKS):
+            for g in range(PASSES):
+                xg = stage_x.tile([P, CHUNK, 4], BF16, name="xg", tag="xg", align_bytes=64)
+                split = V_COLS[c]
+                src = x_raw[(c, g)]
+                if split > 0:
+                    nc.vector.tensor_copy(
+                        out=xg[:, 0:split, :].rearrange("p (c i) t -> p c t i", i=4),
+                        in_=src[:, :, 0:split].rearrange("p t (c i) -> p c t i", i=4),
+                    )
+                nc.scalar.copy(
+                    out=xg[:, split:CHUNK, :].rearrange("p (c i) t -> p c t i", i=4),
+                    in_=src[:, :, split:CHUNK].rearrange("p t (c i) -> p c t i", i=4),
+                )
+                xc = keep.tile([P, CHUNK], U32, name="xc%d_%d" % (c, g), align_bytes=64)
+                xs = keep.tile([P, CHUNK], U8, name="xs%d_%d" % (c, g), align_bytes=64)
+                nc.vector.quantize_mx(
+                    out=xc[:].bitcast(FP8X4), scales=xs[:], in_=xg[:].rearrange("p n t -> p (n t)")
+                )
+                x_codes[(c, g)] = xc
+                x_scales[(c, g)] = xs
+
+        res = [keep.tile([P, CHUNKS * P], F32, name="res%d" % m) for m in range(M_TILES)]
+
+        def mx_pass(acc, m, c, g):
+            nc.tensor.matmul_mx(
+                out=acc[:],
+                lhsT=w_codes[m][:, g * P : (g + 1) * P].bitcast(FP8X4),
+                lhsT_scale=w_scales[m][:, g * P : (g + 1) * P],
+                rhs=x_codes[(c, g)][:].bitcast(FP8X4),
+                rhs_scale=x_scales[(c, g)][:],
+                start=(g == 0),
+                stop=(g == PASSES - 1),
+            )
+
+        def pool_and_store(acc, m, c):
+            nc.vector.tensor_reduce(
+                out=res[m][:, c * P : (c + 1) * P].rearrange("p (i j) -> p i j", i=8),
+                in_=acc[:].rearrange("p (i a j b) -> p i j a b", i=8, a=2, j=16, b=2),
+                axis=mybir.AxisListType.XY,
+                op=mybir.AluOpType.max,
+            )
+            if c == CHUNKS - 1:
+                if m * P < O_KEYS:
+                    dst = keys_out[m * P : (m + 1) * P, :]
+                else:
+                    dst = vals_out[m * P - O_KEYS : (m + 1) * P - O_KEYS, :]
+                nc.sync.dma_start(out=dst, in_=res[m][:])
+
+        first = [psum.tile([P, 512], F32, name="acc", tag="bank") for m in range(FIRST_ROUND)]
+        for g in range(PASSES):
+            for m in range(FIRST_ROUND):
+                mx_pass(first[m], m, 0, g)
+        for m in range(FIRST_ROUND):
+            pool_and_store(first[m], m, 0)
+        for c in range(CHUNKS):
+            for m in range(FIRST_ROUND if c == 0 else 0, M_TILES):
+                acc = psum.tile([P, 512], F32, name="acc", tag="bank")
+                for g in range(PASSES):
+                    mx_pass(acc, m, c, g)
+                pool_and_store(acc, m, c)

@@ -19,7 +19,7 @@ CHUNK = 512
 CHUNKS = 4
 M_TILES = 10
 FIRST_ROUND = 8
-V_COLS = (320, 256, 64, 0)
+V_COLS = (320, 128, 0, 0)
 
 FLOPS = 2 * O_ALL * C_IN * N_PIX
 
@@ -70,10 +70,16 @@ def tile_selfattentionconv2d_pa_kernel(tc, imgs, w_kv, out_0, out_1):
                 for j in range(4):
                     col = (4 * h + j) * P
                     nc.tensor.transpose(bank[:, j * P : (j + 1) * P], words[:, col : col + P], ident[:])
-                nc.scalar.copy(
-                    out=wg_words[:, 2 * h : 2 * h + 2, :, :],
-                    in_=bank[:].rearrange("p (g u o) -> p g o u", g=2, u=2, o=P),
-                )
+                if (2 * m + h) % 4 == 3:
+                    nc.vector.tensor_copy(
+                        out=wg_words[:, 2 * h : 2 * h + 2, :, :],
+                        in_=bank[:].rearrange("p (g u o) -> p g o u", g=2, u=2, o=P),
+                    )
+                else:
+                    nc.scalar.copy(
+                        out=wg_words[:, 2 * h : 2 * h + 2, :, :],
+                        in_=bank[:].rearrange("p (g u o) -> p g o u", g=2, u=2, o=P),
+                    )
             wc = keep.tile([P, PASSES * P], U32, name="wc%d" % m, align_bytes=64)
             ws = keep.tile([P, PASSES * P], U8, name="ws%d" % m, align_bytes=64)
             nc.vector.quantize_mx(out=wc[:].bitcast(FP8X4), scales=ws[:], in_=wg[:])

@@ -18,8 +18,9 @@ PASSES = 4
 CHUNK = 512
 CHUNKS = 4
 M_TILES = 10
+BANKS = 8
 FIRST_ROUND = 8
-V_COLS = (320, 128, 0, 0)
+V_COLS = (352, 128, 0, 0)
 
 FLOPS = 2 * O_ALL * C_IN * N_PIX
 
@@ -38,7 +39,8 @@ def tile_selfattentionconv2d_pa_kernel(tc, imgs, w_kv, out_0, out_1):
         keep = ctx.enter_context(tc.tile_pool(name="keep", bufs=1))
         stage_w = ctx.enter_context(tc.tile_pool(name="stage_w", bufs=3))
         stage_x = ctx.enter_context(tc.tile_pool(name="stage_x", bufs=4))
-        psum = ctx.enter_context(tc.psum_pool(name="psum", bufs=8))
+        psum = ctx.enter_context(tc.psum_pool(name="psum", bufs=1))
+        ctx.enter_context(tc.manual_schedule())
 
         ident = const.tile([P, P], F32, name="ident")
         make_identity(nc, ident[:])
@@ -59,56 +61,57 @@ def tile_selfattentionconv2d_pa_kernel(tc, imgs, w_kv, out_0, out_1):
                     )
                 x_raw[(c, g)] = t
 
-        w_codes = []
-        w_scales = []
-        for m in range(M_TILES):
+        banks_given = [0]
+
+        def next_bank(name):
+            k = banks_given[0]
+            banks_given[0] = k + 1
+            return psum.tile([P, 512], F32, name=name, tag="bank%d" % (k % BANKS))
+
+        w_codes = {}
+        w_scales = {}
+        x_codes = {}
+        x_scales = {}
+
+        def prepare_w(m):
             words = w_raw[m][:].bitcast(F32)
             wg = stage_w.tile([P, C_IN], BF16, name="wg", tag="wg", align_bytes=64)
             wg_words = wg[:].bitcast(F32).rearrange("p (g o u) -> p g o u", g=PASSES, o=P, u=2)
             for h in range(2):
-                bank = psum.tile([P, 512], F32, name="tp", tag="bank")
+                bank = next_bank("tp")
                 for j in range(4):
                     col = (4 * h + j) * P
                     nc.tensor.transpose(bank[:, j * P : (j + 1) * P], words[:, col : col + P], ident[:])
-                if (2 * m + h) % 4 == 3:
-                    nc.vector.tensor_copy(
-                        out=wg_words[:, 2 * h : 2 * h + 2, :, :],
-                        in_=bank[:].rearrange("p (g u o) -> p g o u", g=2, u=2, o=P),
-                    )
-                else:
-                    nc.scalar.copy(
-                        out=wg_words[:, 2 * h : 2 * h + 2, :, :],
-                        in_=bank[:].rearrange("p (g u o) -> p g o u", g=2, u=2, o=P),
-                    )
+                nc.scalar.copy(
+                    out=wg_words[:, 2 * h : 2 * h + 2, :, :],
+                    in_=bank[:].rearrange("p (g u o) -> p g o u", g=2, u=2, o=P),
+                )
             wc = keep.tile([P, PASSES * P], U32, name="wc%d" % m, align_bytes=64)
             ws = keep.tile([P, PASSES * P], U8, name="ws%d" % m, align_bytes=64)
             nc.vector.quantize_mx(out=wc[:].bitcast(FP8X4), scales=ws[:], in_=wg[:])
-            w_codes.append(wc)
-            w_scales.append(ws)
+            w_codes[m] = wc
+            w_scales[m] = ws
 
-        x_codes = {}
-        x_scales = {}
-        for c in range(CHUNKS):
-            for g in range(PASSES):
-                xg = stage_x.tile([P, CHUNK, 4], BF16, name="xg", tag="xg", align_bytes=64)
-                split = V_COLS[c]
-                src = x_raw[(c, g)]
-                if split > 0:
-                    nc.vector.tensor_copy(
-                        out=xg[:, 0:split, :].rearrange("p (c i) t -> p c t i", i=4),
-                        in_=src[:, :, 0:split].rearrange("p t (c i) -> p c t i", i=4),
-                    )
-                nc.scalar.copy(
-                    out=xg[:, split:CHUNK, :].rearrange("p (c i) t -> p c t i", i=4),
-                    in_=src[:, :, split:CHUNK].rearrange("p t (c i) -> p c t i", i=4),
+        def prepare_x(c, g):
+            xg = stage_x.tile([P, CHUNK, 4], BF16, name="xg", tag="xg", align_bytes=64)
+            split = V_COLS[c]
+            src = x_raw[(c, g)]
+            if split > 0:
+                nc.vector.tensor_copy(
+                    out=xg[:, 0:split, :].rearrange("p (c i) t -> p c t i", i=4),
+                    in_=src[:, :, 0:split].rearrange("p t (c i) -> p c t i", i=4),
                 )
-                xc = keep.tile([P, CHUNK], U32, name="xc%d_%d" % (c, g), align_bytes=64)
-                xs = keep.tile([P, CHUNK], U8, name="xs%d_%d" % (c, g), align_bytes=64)
-                nc.vector.quantize_mx(
-                    out=xc[:].bitcast(FP8X4), scales=xs[:], in_=xg[:].rearrange("p n t -> p (n t)")
-                )
-                x_codes[(c, g)] = xc
-                x_scales[(c, g)] = xs
+            nc.scalar.copy(
+                out=xg[:, split:CHUNK, :].rearrange("p (c i) t -> p c t i", i=4),
+                in_=src[:, :, split:CHUNK].rearrange("p t (c i) -> p c t i", i=4),
+            )
+            xc = keep.tile([P, CHUNK], U32, name="xc%d_%d" % (c, g), align_bytes=64)
+            xs = keep.tile([P, CHUNK], U8, name="xs%d_%d" % (c, g), align_bytes=64)
+            nc.vector.quantize_mx(
+                out=xc[:].bitcast(FP8X4), scales=xs[:], in_=xg[:].rearrange("p n t -> p (n t)")
+            )
+            x_codes[(c, g)] = xc
+            x_scales[(c, g)] = xs
 
         res = [keep.tile([P, CHUNKS * P], F32, name="res%d" % m) for m in range(M_TILES)]
 
@@ -130,22 +133,36 @@ def tile_selfattentionconv2d_pa_kernel(tc, imgs, w_kv, out_0, out_1):
                 axis=mybir.AxisListType.XY,
                 op=mybir.AluOpType.max,
             )
+            if m * P < O_KEYS:
+                dst = keys_out[m * P : (m + 1) * P, :]
+            else:
+                dst = vals_out[m * P - O_KEYS : (m + 1) * P - O_KEYS, :]
+            early = (CHUNKS - 1) * P
+            if c == CHUNKS - 2:
+                nc.sync.dma_start(out=dst[:, 0:early], in_=res[m][:, 0:early])
             if c == CHUNKS - 1:
-                if m * P < O_KEYS:
-                    dst = keys_out[m * P : (m + 1) * P, :]
-                else:
-                    dst = vals_out[m * P - O_KEYS : (m + 1) * P - O_KEYS, :]
-                nc.sync.dma_start(out=dst, in_=res[m][:])
+                nc.sync.dma_start(out=dst[:, early : CHUNKS * P], in_=res[m][:, early : CHUNKS * P])
 
-        first = [psum.tile([P, 512], F32, name="acc", tag="bank") for m in range(FIRST_ROUND)]
+        for m in range(FIRST_ROUND):
+            prepare_w(m)
+        for g in range(PASSES):
+            prepare_x(0, g)
+            if FIRST_ROUND + g < M_TILES:
+                prepare_w(FIRST_ROUND + g)
+
+        acc = {}
+        for m in range(FIRST_ROUND):
+            acc[m] = next_bank("acc")
         for g in range(PASSES):
             for m in range(FIRST_ROUND):
-                mx_pass(first[m], m, 0, g)
-        for m in range(FIRST_ROUND):
-            pool_and_store(first[m], m, 0)
+                mx_pass(acc[m], m, 0, g)
+
         for c in range(CHUNKS):
-            for m in range(FIRST_ROUND if c == 0 else 0, M_TILES):
-                acc = psum.tile([P, 512], F32, name="acc", tag="bank")
-                for g in range(PASSES):
-                    mx_pass(acc, m, c, g)
-                pool_and_store(acc, m, c)
+            for m in range(M_TILES):
+                if c + 1 < CHUNKS and m < PASSES:
+                    prepare_x(c + 1, m)
+                if c > 0 or m >= FIRST_ROUND:
+                    acc[m] = next_bank("acc")
+                    for g in range(PASSES):
+                        mx_pass(acc[m], m, c, g)
+                pool_and_store(acc[m], m, c)

@@ -19,8 +19,16 @@ CHUNK = 512
 CHUNKS = 4
 M_TILES = 10
 BANKS = 8
-FIRST_ROUND = 8
-V_COLS = (352, 128, 0, 0)
+HEAD = 5
+V_COLS = ((384, 256, 256, 256), (192,) * 4, (0,) * 4, (0,) * 4)
+TURN_BANKS = 3
+ACC_BANKS = 8 - TURN_BANKS
+TURN_LEAD = 12
+QUANT_W_LEAD = 8
+GROUP_LEAD = 12
+QUANT_X_LEAD = 8
+POOL_LAG = 1
+GOUTER = (0, 1, 2)
 
 FLOPS = 2 * O_ALL * C_IN * N_PIX
 
@@ -37,7 +45,7 @@ def tile_selfattentionconv2d_pa_kernel(tc, imgs, w_kv, out_0, out_1):
         const = ctx.enter_context(tc.tile_pool(name="const", bufs=1))
         raw = ctx.enter_context(tc.tile_pool(name="raw", bufs=1))
         keep = ctx.enter_context(tc.tile_pool(name="keep", bufs=1))
-        stage_w = ctx.enter_context(tc.tile_pool(name="stage_w", bufs=3))
+        stage_w = ctx.enter_context(tc.tile_pool(name="stage_w", bufs=5))
         stage_x = ctx.enter_context(tc.tile_pool(name="stage_x", bufs=4))
         psum = ctx.enter_context(tc.psum_pool(name="psum", bufs=1))
         ctx.enter_context(tc.manual_schedule())
@@ -45,56 +53,86 @@ def tile_selfattentionconv2d_pa_kernel(tc, imgs, w_kv, out_0, out_1):
         ident = const.tile([P, P], F32, name="ident")
         make_identity(nc, ident[:])
 
-        w_raw = []
-        for m in range(M_TILES):
+        w_raw = {}
+        x_raw = {}
+
+        def load_w(m):
             t = raw.tile([P, C_IN], BF16, name="w_raw%d" % m)
             nc.sync.dma_start(out=t[:], in_=w_kv[m * P : (m + 1) * P, :])
-            w_raw.append(t)
-        x_raw = {}
-        for c in range(CHUNKS):
+            w_raw[m] = t
+
+        def load_x(c, g):
+            t = raw.tile([P, 4, CHUNK], BF16, name="x_raw%d_%d" % (c, g))
+            for u in range(2):
+                nc.sync.dma_start(
+                    out=t[:, 2 * u : 2 * u + 2, :],
+                    in_=x_view[g, u, :, :, c * CHUNK : (c + 1) * CHUNK],
+                )
+            x_raw[(c, g)] = t
+
+        for m in range(HEAD):
+            load_w(m)
+        for g in range(PASSES):
+            load_x(0, g)
+        for m in range(HEAD, M_TILES):
+            load_w(m)
+        for c in range(1, CHUNKS):
             for g in range(PASSES):
-                t = raw.tile([P, 4, CHUNK], BF16, name="x_raw%d_%d" % (c, g))
-                for u in range(2):
-                    nc.sync.dma_start(
-                        out=t[:, 2 * u : 2 * u + 2, :],
-                        in_=x_view[g, u, :, :, c * CHUNK : (c + 1) * CHUNK],
-                    )
-                x_raw[(c, g)] = t
+                load_x(c, g)
 
-        banks_given = [0]
+        given = [0, 0]
 
-        def next_bank(name):
-            k = banks_given[0]
-            banks_given[0] = k + 1
-            return psum.tile([P, 512], F32, name=name, tag="bank%d" % (k % BANKS))
+        def turn_bank():
+            k = given[0]
+            given[0] = k + 1
+            return psum.tile([P, 512], F32, name="tp", tag="bank%d" % (HEAD + k % (BANKS - HEAD)))
+
+        def acc_bank():
+            k = given[1]
+            given[1] = k + 1
+            k = k % HEAD if k < M_TILES else (k - M_TILES + HEAD) % BANKS
+            return psum.tile([P, 512], F32, name="acc", tag="bank%d" % k)
 
         w_codes = {}
         w_scales = {}
         x_codes = {}
         x_scales = {}
 
-        def prepare_w(m):
+        w_grouped = {}
+        x_grouped = {}
+
+        turned = {}
+
+        def turn(m):
             words = w_raw[m][:].bitcast(F32)
-            wg = stage_w.tile([P, C_IN], BF16, name="wg", tag="wg", align_bytes=64)
-            wg_words = wg[:].bitcast(F32).rearrange("p (g o u) -> p g o u", g=PASSES, o=P, u=2)
             for h in range(2):
-                bank = next_bank("tp")
+                bank = turn_bank()
                 for j in range(4):
                     col = (4 * h + j) * P
                     nc.tensor.transpose(bank[:, j * P : (j + 1) * P], words[:, col : col + P], ident[:])
+                turned[(m, h)] = bank
+
+        def fetch(m):
+            wg = stage_w.tile([P, C_IN], BF16, name="wg", tag="wg", align_bytes=64)
+            wg_words = wg[:].bitcast(F32).rearrange("p (g o u) -> p g o u", g=PASSES, o=P, u=2)
+            for h in range(2):
                 nc.scalar.copy(
                     out=wg_words[:, 2 * h : 2 * h + 2, :, :],
-                    in_=bank[:].rearrange("p (g u o) -> p g o u", g=2, u=2, o=P),
+                    in_=turned[(m, h)][:].rearrange("p (g u o) -> p g o u", g=2, u=2, o=P),
                 )
+            w_grouped[m] = wg
+
+        def quant_w(m):
+            wg = w_grouped[m]
             wc = keep.tile([P, PASSES * P], U32, name="wc%d" % m, align_bytes=64)
             ws = keep.tile([P, PASSES * P], U8, name="ws%d" % m, align_bytes=64)
             nc.vector.quantize_mx(out=wc[:].bitcast(FP8X4), scales=ws[:], in_=wg[:])
             w_codes[m] = wc
             w_scales[m] = ws
 
-        def prepare_x(c, g):
+        def group_x(c, g):
             xg = stage_x.tile([P, CHUNK, 4], BF16, name="xg", tag="xg", align_bytes=64)
-            split = V_COLS[c]
+            split = V_COLS[c][g]
             src = x_raw[(c, g)]
             if split > 0:
                 nc.vector.tensor_copy(
@@ -105,6 +143,10 @@ def tile_selfattentionconv2d_pa_kernel(tc, imgs, w_kv, out_0, out_1):
                 out=xg[:, split:CHUNK, :].rearrange("p (c i) t -> p c t i", i=4),
                 in_=src[:, :, split:CHUNK].rearrange("p t (c i) -> p c t i", i=4),
             )
+            x_grouped[(c, g)] = xg
+
+        def quant_x(c, g):
+            xg = x_grouped[(c, g)]
             xc = keep.tile([P, CHUNK], U32, name="xc%d_%d" % (c, g), align_bytes=64)
             xs = keep.tile([P, CHUNK], U8, name="xs%d_%d" % (c, g), align_bytes=64)
             nc.vector.quantize_mx(
@@ -143,26 +185,60 @@ def tile_selfattentionconv2d_pa_kernel(tc, imgs, w_kv, out_0, out_1):
             if c == CHUNKS - 1:
                 nc.sync.dma_start(out=dst[:, early : CHUNKS * P], in_=res[m][:, early : CHUNKS * P])
 
-        for m in range(FIRST_ROUND):
-            prepare_w(m)
-        for g in range(PASSES):
-            prepare_x(0, g)
-            if FIRST_ROUND + g < M_TILES:
-                prepare_w(FIRST_ROUND + g)
-
         acc = {}
-        for m in range(FIRST_ROUND):
-            acc[m] = next_bank("acc")
-        for g in range(PASSES):
-            for m in range(FIRST_ROUND):
-                mx_pass(acc[m], m, 0, g)
 
+        def pool(m, c):
+            pool_and_store(acc[m], m, c)
+
+        for m in range(HEAD - 1):
+            turn(m)
+            fetch(m)
+            if m > 0:
+                quant_w(m - 1)
+        turn(HEAD - 1)
+        quant_w(HEAD - 2)
+        group_x(0, 0)
+        quant_x(0, 0)
+        fetch(HEAD - 1)
+        group_x(0, 1)
+        quant_w(HEAD - 1)
+        for g in range(1, PASSES):
+            if g + 1 < PASSES:
+                group_x(0, g + 1)
+            quant_x(0, g)
+
+        order = []
         for c in range(CHUNKS):
-            for m in range(M_TILES):
-                if c + 1 < CHUNKS and m < PASSES:
-                    prepare_x(c + 1, m)
-                if c > 0 or m >= FIRST_ROUND:
-                    acc[m] = next_bank("acc")
-                    for g in range(PASSES):
-                        mx_pass(acc[m], m, c, g)
-                pool_and_store(acc[m], m, c)
+            head = HEAD if c in GOUTER else 0
+            order += [(m, c, g) for g in range(PASSES) for m in range(head)]
+            order += [(m, c, g) for m in range(head, M_TILES) for g in range(PASSES)]
+        due = {}
+
+        def place(i, step, *args):
+            due.setdefault(i, []).append((step, args))
+
+        need_w = {}
+        need_x = {}
+        for i, (m, c, g) in enumerate(order):
+            need_w.setdefault(m, i)
+            need_x.setdefault((c, g), i)
+        for m in range(HEAD, M_TILES):
+            place(need_w[m] - TURN_LEAD, turn, m)
+            place(need_w[m] - TURN_LEAD, fetch, m)
+            place(need_w[m] - QUANT_W_LEAD, quant_w, m)
+        for c in range(1, CHUNKS):
+            for g in range(PASSES):
+                place(need_x[(c, g)] - GROUP_LEAD, group_x, c, g)
+                place(need_x[(c, g)] - QUANT_X_LEAD, quant_x, c, g)
+        for i, (m, c, g) in enumerate(order):
+            if g == PASSES - 1:
+                place(i + POOL_LAG, pool, m, c)
+        for i, (m, c, g) in enumerate(order):
+            for step, args in due.pop(i, []):
+                step(*args)
+            if g == 0:
+                acc[m] = acc_bank()
+            mx_pass(acc[m], m, c, g)
+        for i in sorted(due):
+            for step, args in due[i]:
+                step(*args)

@@ -28,6 +28,7 @@ QUANT_W_LEAD = 8
 GROUP_LEAD = 12
 QUANT_X_LEAD = 8
 POOL_LAG = 1
+WARM = 5
 GOUTER = (0, 1, 2)
 
 FLOPS = 2 * O_ALL * C_IN * N_PIX
@@ -52,6 +53,8 @@ def tile_selfattentionconv2d_pa_kernel(tc, imgs, w_kv, out_0, out_1):
 
         ident = const.tile([P, P], F32, name="ident")
         make_identity(nc, ident[:])
+        idle = const.tile([P, CHUNK], BF16, name="idle")
+        nc.gpsimd.memset(idle[:], 0.0)
 
         w_raw = {}
         x_raw = {}
@@ -196,6 +199,9 @@ def tile_selfattentionconv2d_pa_kernel(tc, imgs, w_kv, out_0, out_1):
             if m > 0:
                 quant_w(m - 1)
         turn(HEAD - 1)
+        spare = turn_bank()
+        for i in range(WARM):
+            nc.tensor.matmul(out=spare[:], lhsT=idle[:, 0:P], rhs=idle[:], start=True, stop=True)
         quant_w(HEAD - 2)
         group_x(0, 0)
         quant_x(0, 0)

@@ -20,14 +20,14 @@ CHUNKS = 4
 M_TILES = 10
 BANKS = 8
 HEAD = 5
-V_COLS = ((384, 256, 256, 256), (192,) * 4, (0,) * 4, (0,) * 4)
+V_COLS = ((384, 224, 224, 224), (192,) * 4, (0,) * 4, (0,) * 4)
 TURN_BANKS = 3
 ACC_BANKS = 8 - TURN_BANKS
-TURN_LEAD = 12
-QUANT_W_LEAD = 8
-GROUP_LEAD = 12
-QUANT_X_LEAD = 8
-POOL_LAG = 1
+TURN_LEAD = 10
+QUANT_W_LEAD = 6
+GROUP_LEAD = 16
+QUANT_X_LEAD = 10
+POOL_LAG = 2
 WARM = 5
 GOUTER = (0, 1, 2)
 
@@ -209,9 +209,9 @@ def tile_selfattentionconv2d_pa_kernel(tc, imgs, w_kv, out_0, out_1):
         group_x(0, 1)
         quant_w(HEAD - 1)
         for g in range(1, PASSES):
+            quant_x(0, g)
             if g + 1 < PASSES:
                 group_x(0, g + 1)
-            quant_x(0, g)
 
         order = []
         for c in range(CHUNKS):

@@ -29,6 +29,7 @@ GROUP_LEAD = 16
 QUANT_X_LEAD = 10
 POOL_LAG = 2
 WARM = 5
+LAST = ((0, 256), (256, 128), (384, 128))
 GOUTER = (0, 1, 2)
 
 FLOPS = 2 * O_ALL * C_IN * N_PIX
@@ -160,21 +161,23 @@ def tile_selfattentionconv2d_pa_kernel(tc, imgs, w_kv, out_0, out_1):
 
         res = [keep.tile([P, CHUNKS * P], F32, name="res%d" % m) for m in range(M_TILES)]
 
-        def mx_pass(acc, m, c, g):
+        def mx_pass(acc, m, c, g, lo=0, wide=CHUNK):
             nc.tensor.matmul_mx(
-                out=acc[:],
+                out=acc[:, 0:wide],
                 lhsT=w_codes[m][:, g * P : (g + 1) * P].bitcast(FP8X4),
                 lhsT_scale=w_scales[m][:, g * P : (g + 1) * P],
-                rhs=x_codes[(c, g)][:].bitcast(FP8X4),
-                rhs_scale=x_scales[(c, g)][:],
+                rhs=x_codes[(c, g)][:, lo : lo + wide].bitcast(FP8X4),
+                rhs_scale=x_scales[(c, g)][:, lo : lo + wide],
                 start=(g == 0),
                 stop=(g == PASSES - 1),
             )
 
-        def pool_and_store(acc, m, c):
+        def pool_and_store(acc, m, c, lo=0, wide=CHUNK):
+            first = c * P + lo // 4
+            last = first + wide // 4
             nc.vector.tensor_reduce(
-                out=res[m][:, c * P : (c + 1) * P].rearrange("p (i j) -> p i j", i=8),
-                in_=acc[:].rearrange("p (i a j b) -> p i j a b", i=8, a=2, j=16, b=2),
+                out=res[m][:, first:last].rearrange("p (i j) -> p i j", j=16),
+                in_=acc[:, 0:wide].rearrange("p (i a j b) -> p i j a b", a=2, j=16, b=2),
                 axis=mybir.AxisListType.XY,
                 op=mybir.AluOpType.max,
             )
@@ -182,11 +185,10 @@ def tile_selfattentionconv2d_pa_kernel(tc, imgs, w_kv, out_0, out_1):
                 dst = keys_out[m * P : (m + 1) * P, :]
             else:
                 dst = vals_out[m * P - O_KEYS : (m + 1) * P - O_KEYS, :]
-            early = (CHUNKS - 1) * P
             if c == CHUNKS - 2:
-                nc.sync.dma_start(out=dst[:, 0:early], in_=res[m][:, 0:early])
+                nc.sync.dma_start(out=dst[:, 0:last], in_=res[m][:, 0:last])
             if c == CHUNKS - 1:
-                nc.sync.dma_start(out=dst[:, early : CHUNKS * P], in_=res[m][:, early : CHUNKS * P])
+                nc.sync.dma_start(out=dst[:, first:last], in_=res[m][:, first:last])
 
         acc = {}
 
@@ -237,9 +239,9 @@ def tile_selfattentionconv2d_pa_kernel(tc, imgs, w_kv, out_0, out_1):
                 place(need_x[(c, g)] - GROUP_LEAD, group_x, c, g)
                 place(need_x[(c, g)] - QUANT_X_LEAD, quant_x, c, g)
         for i, (m, c, g) in enumerate(order):
-            if g == PASSES - 1:
+            if g == PASSES - 1 and i + 1 < len(order):
                 place(i + POOL_LAG, pool, m, c)
-        for i, (m, c, g) in enumerate(order):
+        for i, (m, c, g) in enumerate(order[:-PASSES]):
             for step, args in due.pop(i, []):
                 step(*args)
             if g == 0:
@@ -248,3 +250,9 @@ def tile_selfattentionconv2d_pa_kernel(tc, imgs, w_kv, out_0, out_1):
         for i in sorted(due):
             for step, args in due[i]:
                 step(*args)
+        m, c, g = order[-1]
+        for lo, wide in LAST:
+            bank = acc_bank()
+            for g in range(PASSES):
+                mx_pass(bank, m, c, g, lo, wide)
+            pool_and_store(bank, m, c, lo, wide)

@@ -29,6 +29,9 @@ GROUP_LEAD = 16
 QUANT_X_LEAD = 10
 POOL_LAG = 2
 WARM = 5
+WS_AT = 64
+XC_AT = 32
+XS_AT = 192
 LAST = ((0, 256), (256, 128), (384, 128))
 GOUTER = (0, 1, 2)
 
@@ -46,8 +49,9 @@ def tile_selfattentionconv2d_pa_kernel(tc, imgs, w_kv, out_0, out_1):
     with ExitStack() as ctx:
         const = ctx.enter_context(tc.tile_pool(name="const", bufs=1))
         raw = ctx.enter_context(tc.tile_pool(name="raw", bufs=1))
+        raw_x = ctx.enter_context(tc.tile_pool(name="raw_x", bufs=12))
         keep = ctx.enter_context(tc.tile_pool(name="keep", bufs=1))
-        stage_w = ctx.enter_context(tc.tile_pool(name="stage_w", bufs=5))
+        stage_w = ctx.enter_context(tc.tile_pool(name="stage_w", bufs=4))
         stage_x = ctx.enter_context(tc.tile_pool(name="stage_x", bufs=4))
         psum = ctx.enter_context(tc.psum_pool(name="psum", bufs=1))
         ctx.enter_context(tc.manual_schedule())
@@ -66,7 +70,7 @@ def tile_selfattentionconv2d_pa_kernel(tc, imgs, w_kv, out_0, out_1):
             w_raw[m] = t
 
         def load_x(c, g):
-            t = raw.tile([P, 4, CHUNK], BF16, name="x_raw%d_%d" % (c, g))
+            t = raw_x.tile([P, 4, CHUNK], BF16, name="x_raw", tag="x_raw")
             for u in range(2):
                 nc.sync.dma_start(
                     out=t[:, 2 * u : 2 * u + 2, :],
@@ -128,11 +132,11 @@ def tile_selfattentionconv2d_pa_kernel(tc, imgs, w_kv, out_0, out_1):
 
         def quant_w(m):
             wg = w_grouped[m]
-            wc = keep.tile([P, PASSES * P], U32, name="wc%d" % m, align_bytes=64)
-            ws = keep.tile([P, PASSES * P], U8, name="ws%d" % m, align_bytes=64)
-            nc.vector.quantize_mx(out=wc[:].bitcast(FP8X4), scales=ws[:], in_=wg[:])
+            wc = keep.tile([P, PASSES * P], U32, name="wc%d" % m, align_bytes=256)
+            ws = keep.tile([P, WS_AT + PASSES * P], U8, name="ws%d" % m, align_bytes=256)
+            nc.vector.quantize_mx(out=wc[:].bitcast(FP8X4), scales=ws[:, WS_AT:], in_=wg[:])
             w_codes[m] = wc
-            w_scales[m] = ws
+            w_scales[m] = ws[:, WS_AT:]
 
         def group_x(c, g):
             xg = stage_x.tile([P, CHUNK, 4], BF16, name="xg", tag="xg", align_bytes=64)
@@ -151,13 +155,15 @@ def tile_selfattentionconv2d_pa_kernel(tc, imgs, w_kv, out_0, out_1):
 
         def quant_x(c, g):
             xg = x_grouped[(c, g)]
-            xc = keep.tile([P, CHUNK], U32, name="xc%d_%d" % (c, g), align_bytes=64)
-            xs = keep.tile([P, CHUNK], U8, name="xs%d_%d" % (c, g), align_bytes=64)
+            xc = keep.tile([P, XC_AT + CHUNK], U32, name="xc%d_%d" % (c, g), align_bytes=256)
+            xs = keep.tile([P, XS_AT + CHUNK], U8, name="xs%d_%d" % (c, g), align_bytes=256)
             nc.vector.quantize_mx(
-                out=xc[:].bitcast(FP8X4), scales=xs[:], in_=xg[:].rearrange("p n t -> p (n t)")
+                out=xc[:, XC_AT:].bitcast(FP8X4),
+                scales=xs[:, XS_AT:],
+                in_=xg[:].rearrange("p n t -> p (n t)"),
             )
-            x_codes[(c, g)] = xc
-            x_scales[(c, g)] = xs
+            x_codes[(c, g)] = xc[:, XC_AT:]
+            x_scales[(c, g)] = xs[:, XS_AT:]
 
         res = [keep.tile([P, CHUNKS * P], F32, name="res%d" % m) for m in range(M_TILES)]
 

@@ -30,7 +30,7 @@ QUANT_X_LEAD = 10
 POOL_LAG = 2
 WARM = 5
 WS_AT = 64
-XC_AT = 32
+XC_AT = 16
 XS_AT = 192
 LAST = ((0, 256), (256, 128), (384, 128))
 GOUTER = (0, 1, 2)

@@ -20,12 +20,12 @@ CHUNKS = 4
 M_TILES = 10
 BANKS = 8
 HEAD = 5
-V_COLS = ((384, 224, 224, 224), (192,) * 4, (0,) * 4, (0,) * 4)
+V_COLS = ((320, 256, 256, 256), (128,) * 4, (0,) * 4, (0,) * 4)
 TURN_BANKS = 3
 ACC_BANKS = 8 - TURN_BANKS
-TURN_LEAD = 10
-QUANT_W_LEAD = 6
-GROUP_LEAD = 16
+TURN_LEAD = 12
+QUANT_W_LEAD = 7
+GROUP_LEAD = 18
 QUANT_X_LEAD = 10
 POOL_LAG = 2
 WARM = 5
@@ -120,23 +120,26 @@ def tile_selfattentionconv2d_pa_kernel(tc, imgs, w_kv, out_0, out_1):
                     nc.tensor.transpose(bank[:, j * P : (j + 1) * P], words[:, col : col + P], ident[:])
                 turned[(m, h)] = bank
 
-        def fetch(m):
+        def fetch(m, second=nc.scalar.copy):
             wg = stage_w.tile([P, C_IN], BF16, name="wg", tag="wg", align_bytes=64)
             wg_words = wg[:].bitcast(F32).rearrange("p (g o u) -> p g o u", g=PASSES, o=P, u=2)
-            for h in range(2):
-                nc.scalar.copy(
+            for h, move in ((0, nc.scalar.copy), (1, second)):
+                move(
                     out=wg_words[:, 2 * h : 2 * h + 2, :, :],
                     in_=turned[(m, h)][:].rearrange("p (g u o) -> p g o u", g=2, u=2, o=P),
                 )
             w_grouped[m] = wg
 
-        def quant_w(m):
-            wg = w_grouped[m]
-            wc = keep.tile([P, PASSES * P], U32, name="wc%d" % m, align_bytes=256)
-            ws = keep.tile([P, WS_AT + PASSES * P], U8, name="ws%d" % m, align_bytes=256)
-            nc.vector.quantize_mx(out=wc[:].bitcast(FP8X4), scales=ws[:, WS_AT:], in_=wg[:])
-            w_codes[m] = wc
-            w_scales[m] = ws[:, WS_AT:]
+        def quant_w(m, lo=0, hi=PASSES):
+            if lo == 0:
+                w_codes[m] = keep.tile([P, PASSES * P], U32, name="wc%d" % m, align_bytes=256)
+                ws = keep.tile([P, WS_AT + PASSES * P], U8, name="ws%d" % m, align_bytes=256)
+                w_scales[m] = ws[:, WS_AT:]
+            nc.vector.quantize_mx(
+                out=w_codes[m][:, lo * P : hi * P].bitcast(FP8X4),
+                scales=w_scales[m][:, lo * P : hi * P],
+                in_=w_grouped[m][:, 4 * lo * P : 4 * hi * P],
+            )
 
         def group_x(c, g):
             xg = stage_x.tile([P, CHUNK, 4], BF16, name="xg", tag="xg", align_bytes=64)
@@ -203,15 +206,15 @@ def tile_selfattentionconv2d_pa_kernel(tc, imgs, w_kv, out_0, out_1):
 
         for m in range(HEAD - 1):
             turn(m)
-            fetch(m)
+            fetch(m, nc.vector.tensor_copy if m % 2 == 0 else nc.scalar.copy)
             if m > 0:
                 quant_w(m - 1)
         turn(HEAD - 1)
         spare = turn_bank()
         for i in range(WARM):
             nc.tensor.matmul(out=spare[:], lhsT=idle[:, 0:P], rhs=idle[:], start=True, stop=True)
-        quant_w(HEAD - 2)
         group_x(0, 0)
+        quant_w(HEAD - 2)
         quant_x(0, 0)
         fetch(HEAD - 1)
         group_x(0, 1)
@@ -239,7 +242,8 @@ def tile_selfattentionconv2d_pa_kernel(tc, imgs, w_kv, out_0, out_1):
         for m in range(HEAD, M_TILES):
             place(need_w[m] - TURN_LEAD, turn, m)
             place(need_w[m] - TURN_LEAD, fetch, m)
-            place(need_w[m] - QUANT_W_LEAD, quant_w, m)
+            place(need_w[m] - QUANT_W_LEAD, quant_w, m, 0, 2)
+            place(need_w[m] - QUANT_W_LEAD + 1, quant_w, m, 2, PASSES)
         for c in range(1, CHUNKS):
             for g in range(PASSES):
                 place(need_x[(c, g)] - GROUP_LEAD, group_x, c, g)

@@ -29,7 +29,7 @@ GROUP_LEAD = 18
 QUANT_X_LEAD = 10
 POOL_LAG = 2
 WARM = 5
-WS_AT = 64
+WS_AT = 0
 XC_AT = 16
 XS_AT = 192
 LAST = ((0, 256), (256, 128), (384, 128))

@@ -228,7 +228,13 @@ def tile_selfattentionconv2d_pa_kernel(tc, imgs, w_kv, out_0, out_1):
         for c in range(CHUNKS):
             head = HEAD if c in GOUTER else 0
             order += [(m, c, g) for g in range(PASSES) for m in range(head)]
-            order += [(m, c, g) for m in range(head, M_TILES) for g in range(PASSES)]
+            if c == 0:
+                order += [(m, c, g) for m in range(head, M_TILES) for g in range(PASSES)]
+            else:
+                alone = M_TILES - 2 if c == CHUNKS - 1 else M_TILES - 1
+                for m in range(head, alone, 2):
+                    order += [(n, c, g) for g in range(PASSES) for n in (m, m + 1)]
+                order += [(m, c, g) for m in range(alone, M_TILES) for g in range(PASSES)]
         due = {}
 
         def place(i, step, *args):

from contextlib import ExitStack

import concourse.mybir as mybir
from concourse.masks import make_identity

F32 = mybir.dt.float32
BF16 = mybir.dt.bfloat16
U32 = mybir.dt.uint32
U8 = mybir.dt.uint8
FP8X4 = mybir.dt.float8_e4m3fn_x4

P = 128
C_IN = 2048
N_PIX = 2048
O_ALL = 1280
O_KEYS = 256
PASSES = 4
CHUNK = 512
CHUNKS = 4
M_TILES = 10
BANKS = 8
HEAD = 5
V_COLS = ((320, 256, 256, 256), (128,) * 4, (0,) * 4, (0,) * 4)
TURN_BANKS = 3
ACC_BANKS = 8 - TURN_BANKS
TURN_LEAD = 12
QUANT_W_LEAD = 7
GROUP_LEAD = 18
QUANT_X_LEAD = 10
POOL_LAG = 2
WARM = 5
WS_AT = 0
XC_AT = 16
XS_AT = 192
LAST = ((0, 256), (256, 128), (384, 128))
GOUTER = (0, 1, 2)

FLOPS = 2 * O_ALL * C_IN * N_PIX


def tile_selfattentionconv2d_pa_kernel(tc, imgs, w_kv, out_0, out_1):
    nc = tc.nc
    x_view = imgs.rearrange("b c h w -> (b c) (h w)").rearrange(
        "(g u q e) n -> g u q e n", g=PASSES, u=2, q=P, e=2
    )
    keys_out = out_0.rearrange("b o i j -> (b o) (i j)")
    vals_out = out_1.rearrange("b o i j -> (b o) (i j)")

    with ExitStack() as ctx:
        const = ctx.enter_context(tc.tile_pool(name="const", bufs=1))
        raw = ctx.enter_context(tc.tile_pool(name="raw", bufs=1))
        raw_x = ctx.enter_context(tc.tile_pool(name="raw_x", bufs=12))
        keep = ctx.enter_context(tc.tile_pool(name="keep", bufs=1))
        stage_w = ctx.enter_context(tc.tile_pool(name="stage_w", bufs=4))
        stage_x = ctx.enter_context(tc.tile_pool(name="stage_x", bufs=4))
        psum = ctx.enter_context(tc.psum_pool(name="psum", bufs=1))
        ctx.enter_context(tc.manual_schedule())

        ident = const.tile([P, P], F32, name="ident")
        make_identity(nc, ident[:])
        idle = const.tile([P, CHUNK], BF16, name="idle")
        nc.gpsimd.memset(idle[:], 0.0)

        w_raw = {}
        x_raw = {}

        def load_w(m):
            t = raw.tile([P, C_IN], BF16, name="w_raw%d" % m)
            nc.sync.dma_start(out=t[:], in_=w_kv[m * P : (m + 1) * P, :])
            w_raw[m] = t

        def load_x(c, g):
            t = raw_x.tile([P, 4, CHUNK], BF16, name="x_raw", tag="x_raw")
            for u in range(2):
                nc.sync.dma_start(
                    out=t[:, 2 * u : 2 * u + 2, :],
                    in_=x_view[g, u, :, :, c * CHUNK : (c + 1) * CHUNK],
                )
            x_raw[(c, g)] = t

        for m in range(HEAD):
            load_w(m)
        for g in range(PASSES):
            load_x(0, g)
        for m in range(HEAD, M_TILES):
            load_w(m)
        for c in range(1, CHUNKS):
            for g in range(PASSES):
                load_x(c, g)

        given = [0, 0]

        def turn_bank():
            k = given[0]
            given[0] = k + 1
            return psum.tile([P, 512], F32, name="tp", tag="bank%d" % (HEAD + k % (BANKS - HEAD)))

        def acc_bank():
            k = given[1]
            given[1] = k + 1
            k = k % HEAD if k < M_TILES else (k - M_TILES + HEAD) % BANKS
            return psum.tile([P, 512], F32, name="acc", tag="bank%d" % k)

        w_codes = {}
        w_scales = {}
        x_codes = {}
        x_scales = {}

        w_grouped = {}
        x_grouped = {}

        turned = {}

        def turn(m):
            words = w_raw[m][:].bitcast(F32)
            for h in range(2):
                bank = turn_bank()
                for j in range(4):
                    col = (4 * h + j) * P
                    nc.tensor.transpose(bank[:, j * P : (j + 1) * P], words[:, col : col + P], ident[:])
                turned[(m, h)] = bank

        def fetch(m, second=nc.scalar.copy):
            wg = stage_w.tile([P, C_IN], BF16, name="wg", tag="wg", align_bytes=64)
            wg_words = wg[:].bitcast(F32).rearrange("p (g o u) -> p g o u", g=PASSES, o=P, u=2)
            for h, move in ((0, nc.scalar.copy), (1, second)):
                move(
                    out=wg_words[:, 2 * h : 2 * h + 2, :, :],
                    in_=turned[(m, h)][:].rearrange("p (g u o) -> p g o u", g=2, u=2, o=P),
                )
            w_grouped[m] = wg

        def quant_w(m, lo=0, hi=PASSES):
            if lo == 0:
                w_codes[m] = keep.tile([P, PASSES * P], U32, name="wc%d" % m, align_bytes=256)
                ws = keep.tile([P, WS_AT + PASSES * P], U8, name="ws%d" % m, align_bytes=256)
                w_scales[m] = ws[:, WS_AT:]
            nc.vector.quantize_mx(
                out=w_codes[m][:, lo * P : hi * P].bitcast(FP8X4),
                scales=w_scales[m][:, lo * P : hi * P],
                in_=w_grouped[m][:, 4 * lo * P : 4 * hi * P],
            )

        def group_x(c, g):
            xg = stage_x.tile([P, CHUNK, 4], BF16, name="xg", tag="xg", align_bytes=64)
            split = V_COLS[c][g]
            src = x_raw[(c, g)]
            if split > 0:
                nc.vector.tensor_copy(
                    out=xg[:, 0:split, :].rearrange("p (c i) t -> p c t i", i=4),
                    in_=src[:, :, 0:split].rearrange("p t (c i) -> p c t i", i=4),
                )
            nc.scalar.copy(
                out=xg[:, split:CHUNK, :].rearrange("p (c i) t -> p c t i", i=4),
                in_=src[:, :, split:CHUNK].rearrange("p t (c i) -> p c t i", i=4),
            )
            x_grouped[(c, g)] = xg

        def quant_x(c, g):
            xg = x_grouped[(c, g)]
            xc = keep.tile([P, XC_AT + CHUNK], U32, name="xc%d_%d" % (c, g), align_bytes=256)
            xs = keep.tile([P, XS_AT + CHUNK], U8, name="xs%d_%d" % (c, g), align_bytes=256)
            nc.vector.quantize_mx(
                out=xc[:, XC_AT:].bitcast(FP8X4),
                scales=xs[:, XS_AT:],
                in_=xg[:].rearrange("p n t -> p (n t)"),
            )
            x_codes[(c, g)] = xc[:, XC_AT:]
            x_scales[(c, g)] = xs[:, XS_AT:]

        res = [keep.tile([P, CHUNKS * P], F32, name="res%d" % m) for m in range(M_TILES)]

        def mx_pass(acc, m, c, g, lo=0, wide=CHUNK):
            nc.tensor.matmul_mx(
                out=acc[:, 0:wide],
                lhsT=w_codes[m][:, g * P : (g + 1) * P].bitcast(FP8X4),
                lhsT_scale=w_scales[m][:, g * P : (g + 1) * P],
                rhs=x_codes[(c, g)][:, lo : lo + wide].bitcast(FP8X4),
                rhs_scale=x_scales[(c, g)][:, lo : lo + wide],
                start=(g == 0),
                stop=(g == PASSES - 1),
            )

        def pool_and_store(acc, m, c, lo=0, wide=CHUNK):
            first = c * P + lo // 4
            last = first + wide // 4
            nc.vector.tensor_reduce(
                out=res[m][:, first:last].rearrange("p (i j) -> p i j", j=16),
                in_=acc[:, 0:wide].rearrange("p (i a j b) -> p i j a b", a=2, j=16, b=2),
                axis=mybir.AxisListType.XY,
                op=mybir.AluOpType.max,
            )
            if m * P < O_KEYS:
                dst = keys_out[m * P : (m + 1) * P, :]
            else:
                dst = vals_out[m * P - O_KEYS : (m + 1) * P - O_KEYS, :]
            if c == CHUNKS - 2:
                nc.sync.dma_start(out=dst[:, 0:last], in_=res[m][:, 0:last])
            if c == CHUNKS - 1:
                nc.sync.dma_start(out=dst[:, first:last], in_=res[m][:, first:last])

        acc = {}

        def pool(m, c):
            pool_and_store(acc[m], m, c)

        for m in range(HEAD - 1):
            turn(m)
            fetch(m, nc.vector.tensor_copy if m % 2 == 0 else nc.scalar.copy)
            if m > 0:
                quant_w(m - 1)
        turn(HEAD - 1)
        spare = turn_bank()
        for i in range(WARM):
            nc.tensor.matmul(out=spare[:], lhsT=idle[:, 0:P], rhs=idle[:], start=True, stop=True)
        group_x(0, 0)
        quant_w(HEAD - 2)
        quant_x(0, 0)
        fetch(HEAD - 1)
        group_x(0, 1)
        quant_w(HEAD - 1)
        for g in range(1, PASSES):
            quant_x(0, g)
            if g + 1 < PASSES:
                group_x(0, g + 1)

        order = []
        for c in range(CHUNKS):
            head = HEAD if c in GOUTER else 0
            order += [(m, c, g) for g in range(PASSES) for m in range(head)]
            if c == 0:
                order += [(m, c, g) for m in range(head, M_TILES) for g in range(PASSES)]
            else:
                alone = M_TILES - 2 if c == CHUNKS - 1 else M_TILES - 1
                for m in range(head, alone, 2):
                    order += [(n, c, g) for g in range(PASSES) for n in (m, m + 1)]
                order += [(m, c, g) for m in range(alone, M_TILES) for g in range(PASSES)]
        due = {}

        def place(i, step, *args):
            due.setdefault(i, []).append((step, args))

        need_w = {}
        need_x = {}
        for i, (m, c, g) in enumerate(order):
            need_w.setdefault(m, i)
            need_x.setdefault((c, g), i)
        for m in range(HEAD, M_TILES):
            place(need_w[m] - TURN_LEAD, turn, m)
            place(need_w[m] - TURN_LEAD, fetch, m)
            place(need_w[m] - QUANT_W_LEAD, quant_w, m, 0, 2)
            place(need_w[m] - QUANT_W_LEAD + 1, quant_w, m, 2, PASSES)
        for c in range(1, CHUNKS):
            for g in range(PASSES):
                place(need_x[(c, g)] - GROUP_LEAD, group_x, c, g)
                place(need_x[(c, g)] - QUANT_X_LEAD, quant_x, c, g)
        for i, (m, c, g) in enumerate(order):
            if g == PASSES - 1 and i + 1 < len(order):
                place(i + POOL_LAG, pool, m, c)
        for i, (m, c, g) in enumerate(order[:-PASSES]):
            for step, args in due.pop(i, []):
                step(*args)
            if g == 0:
                acc[m] = acc_bank()
            mx_pass(acc[m], m, c, g)
        for i in sorted(due):
            for step, args in due[i]:
                step(*args)
        m, c, g = order[-1]
        for lo, wide in LAST:
            bank = acc_bank()
            for g in range(PASSES):
                mx_pass(bank, m, c, g, lo, wide)
            pool_and_store(bank, m, c, lo, wide)
